import numpy as np
import ml_dtypes


def mxq(x, axis, fmt="e4m3"):
    dtype, down = {"e4m3": (ml_dtypes.float8_e4m3fn, 7), "e5m2": (ml_dtypes.float8_e5m2, 14)}[fmt]
    v = np.moveaxis(np.asarray(x, np.float32).astype(ml_dtypes.bfloat16).astype(np.float64), axis, -1)
    blocks = v.reshape(v.shape[:-1] + (-1, 32))
    amax = np.abs(blocks).max(-1, keepdims=True)
    byte = np.maximum(np.where(amax > 0, np.frexp(amax)[1] - 1 + 127, 0) - down, 1)
    scale = np.exp2(byte - 127.0)
    codes = (blocks / scale).astype(np.float32).astype(dtype).astype(np.float64)
    return np.moveaxis((codes * scale).reshape(v.shape), -1, axis)


WIDE = False


def mx_kscale(k):
    if not WIDE:
        return np.ones(k)
    levels = np.array([10, -10, 5, -5, 0])
    a = np.random.permutation(np.resize(levels, k // 512 * 4)).reshape(k // 512, 4)
    idx = np.arange(k)
    return np.exp2(a[idx // 512, idx % 128 // 32])


BF16 = ml_dtypes.bfloat16


def bf(x):
    return np.asarray(x, np.float32).astype(BF16)


def f64(x):
    return np.asarray(x).astype(np.float64)


E2M1 = np.array([0.0, 0.5, 1.0, 1.5, 2.0, 3.0, 4.0, 6.0, -0.0, -0.5, -1.0, -1.5, -2.0, -3.0, -4.0, -6.0])


def pack_weight(w, fmt):
    k, n = w.shape
    w = f64(bf(w)).reshape(k // 32, 32, n)
    amax = np.abs(w).max(1)
    if fmt == "e4m3":
        byte = np.frexp(amax)[1] - 1 + 127 - 7
    else:
        mant, ex = np.frexp(amax / 6.0)
        byte = np.where(mant > 0.5, ex, ex - 1) + 127
    byte = np.clip(np.where(amax > 0, byte, 1), 1, 254)
    scaled = (w * np.exp2(127.0 - byte)[:, None, :]).reshape(k, n).astype(np.float32)
    by_word = np.ascontiguousarray(scaled.reshape(k // 512, 128, 4, n).transpose(0, 1, 3, 2))
    if fmt == "e4m3":
        words = by_word.astype(ml_dtypes.float8_e4m3fn).view(np.uint8)
    else:
        c = by_word.astype(ml_dtypes.float4_e2m1fn).view(np.uint8) & 0xF
        words = c[..., 0::2] | (c[..., 1::2] << 4)
    return np.ascontiguousarray(words), np.ascontiguousarray(byte.astype(np.uint8).reshape(k // 512, 16, n))


def unpack_weight(words, scales, fmt):
    g, p, n, _ = words.shape
    if fmt == "e4m3":
        vals = np.ascontiguousarray(words).view(ml_dtypes.float8_e4m3fn).astype(np.float64)
    else:
        nib = np.empty((g, p, n, 4), np.uint8)
        nib[..., 0::2] = words & 0xF
        nib[..., 1::2] = words >> 4
        vals = E2M1[nib]
    vals = vals * np.repeat(np.exp2(scales.astype(np.float64) - 127.0), 8, axis=1)[..., None]
    return vals.transpose(0, 1, 3, 2).reshape(g * 512, n)

def pack4(w):
    words, scales = pack_weight(w, "e2m1")
    return words.reshape(words.shape[0], 128, -1), scales


def unpack4(words, scales):
    return unpack_weight(words.reshape(words.shape[0], 128, -1, 2), scales, "e2m1")


B, D_IN, D_H, W_RANK, U_RANK = 4096, 1024, 1024, 512, 512


def sigmoid(v):
    return 1.0 / (1.0 + np.exp(-v))


def setup_inputs():
    s, t = mx_kscale(W_RANK), mx_kscale(U_RANK)
    wx_r = bf(np.random.standard_normal((B, W_RANK)) * s)
    uh_r = bf(np.random.standard_normal((B, U_RANK)) * t)
    state = bf(np.random.standard_normal((B, D_H)))
    W2 = np.random.standard_normal((D_H, W_RANK)) * 0.7 / np.sqrt(W_RANK) / s
    U2 = np.random.standard_normal((D_H, U_RANK)) * 0.7 / np.sqrt(U_RANK) / t
    W2_words, W2_scales = pack4(np.ascontiguousarray(W2.T))
    U2_words, U2_scales = pack4(np.ascontiguousarray(U2.T))
    return {
        "wx_r": wx_r,
        "uh_r": uh_r,
        "state": state,
        "W2_words": W2_words,
        "W2_scales": W2_scales,
        "U2_words": U2_words,
        "U2_scales": U2_scales,
        "bias_gate": bf(1.0 + 0.5 * np.random.standard_normal((1, D_H))),
        "bias_update": bf(1.0 + 0.5 * np.random.standard_normal((1, D_H))),
        "zeta": bf(1.0 + 0.1 * np.random.standard_normal((1, 1))),
        "nu": bf(-1.5 + 0.1 * np.random.standard_normal((1, 1))),
    }


def reference(wx_r, uh_r, state, W2_words, W2_scales, U2_words, U2_scales, bias_gate, bias_update, zeta, nu):
    wx = mxq(f64(wx_r), 1, "e4m3") @ unpack4(W2_words, W2_scales)
    uh = mxq(f64(uh_r), 1, "e4m3") @ unpack4(U2_words, U2_scales)
    pre = wx + uh
    z = sigmoid(pre + f64(bias_gate))
    h_cand = np.tanh(pre + f64(bias_update))
    return z * f64(state) + (sigmoid(f64(zeta)) * (1.0 - z) + sigmoid(f64(nu))) * h_cand

@@ -1,0 +1,304 @@
+from contextlib import ExitStack
+
+import concourse.mybir as mybir
+from concourse.masks import make_identity
+
+F32 = mybir.dt.float32
+BF16 = mybir.dt.bfloat16
+I32 = mybir.dt.int32
+U32 = mybir.dt.uint32
+U8 = mybir.dt.uint8
+FP8X4 = mybir.dt.float8_e4m3fn_x4
+FP4X4 = mybir.dt.float4_e2m1fn_x4
+ACT = mybir.ActivationFunctionType
+ALU = mybir.AluOpType
+
+P = 128
+BATCH = 4096
+RANK = 512
+D_H = 1024
+WORDS = RANK // 2
+GROUP = 512
+ROWS = GROUP // P
+N_GROUPS = BATCH // GROUP
+HALF = 512
+TILES = HALF // P
+HALVES = D_H // HALF
+N_UNITS = N_GROUPS * HALVES
+N_STEPS = 2 * N_GROUPS
+STEP_LEAD = 3
+GPSIMD_TILES = 3
+TINY = 1e-30
+
+FLOPS = 2 * BATCH * D_H * 2 * RANK
+
+
+def tile_fastgrnncudacell_pa_t_kernel(
+    tc,
+    wx_r,
+    uh_r,
+    state,
+    W2_words,
+    W2_scales,
+    U2_words,
+    U2_scales,
+    bias_gate,
+    bias_update,
+    zeta,
+    nu,
+    out,
+):
+    nc = tc.nc
+    with ExitStack() as stack:
+        consts = stack.enter_context(tc.tile_pool(name="consts", bufs=1))
+        x_pool = stack.enter_context(tc.tile_pool(name="x", bufs=6))
+        state_pool = stack.enter_context(tc.tile_pool(name="state", bufs=3))
+        out_pool = stack.enter_context(tc.tile_pool(name="out", bufs=2))
+        grouped_pool = stack.enter_context(tc.tile_pool(name="grouped", bufs=2))
+        code_pool = stack.enter_context(tc.tile_pool(name="codes", bufs=4))
+        feature_pool = stack.enter_context(tc.tile_pool(name="feature_major", bufs=2))
+        acc_banks = stack.enter_context(tc.psum_pool(name="acc", bufs=3))
+        flip_banks = stack.enter_context(tc.psum_pool(name="flip", bufs=5))
+        stack.enter_context(tc.manual_schedule())
+
+        x_tiles = {}
+        grouped_tiles = {}
+        quantised = {}
+        state_tiles = {}
+        out_tiles = {}
+        z_tiles = {}
+        c_tiles = {}
+        p_tiles = {}
+
+        def group_rows(dram, group):
+            rows = dram[group * GROUP : (group + 1) * GROUP, :]
+            return rows.rearrange("(p j) c -> p j c", j=ROWS)
+
+        def load_x(group):
+            for operand, source in enumerate((wx_r, uh_r)):
+                x_sb = x_pool.tile([P, ROWS, RANK], BF16)
+                nc.sync.dma_start(out=x_sb[:], in_=group_rows(source, group))
+                x_tiles[2 * group + operand] = x_sb
+
+        def load_state(group):
+            state_sb = state_pool.tile([P, ROWS, D_H], BF16)
+            nc.sync.dma_start(out=state_sb[:], in_=group_rows(state, group))
+            state_tiles[group] = state_sb
+
+        w_planes = consts.tile([P, 2, D_H], U8, align_bytes=64)
+        nc.vector.memset(w_planes[:].rearrange("p o n -> p (o n)").bitcast(I32), 0)
+        bias_rows = consts.tile([P, P], BF16)
+        nc.vector.memset(bias_rows[:], 0.0)
+        ident = consts.tile([P, P], F32)
+        make_identity(nc, ident[:])
+
+        load_x(0)
+        w_words = consts.tile([P, 2, 2 * D_H], U8, align_bytes=64)
+        for operand, (words, scales) in enumerate(((W2_words, W2_scales), (U2_words, U2_scales))):
+            nc.sync.dma_start(out=w_words[:, operand, :].bitcast(I32), in_=words[0].bitcast(I32))
+            for quadrant in range(4):
+                nc.sync.dma_start(
+                    out=w_planes[32 * quadrant : 32 * quadrant + 4, operand, :].bitcast(I32),
+                    in_=scales[0, 4 * quadrant : 4 * quadrant + 4, :].bitcast(I32),
+                )
+        load_x(1)
+        load_state(0)
+        load_x(2)
+
+        nc.scalar.dma_start(
+            out=bias_rows[0 : D_H // P, :], in_=bias_gate.rearrange("o (m p) -> (o m) p", p=P)
+        )
+        nc.scalar.dma_start(
+            out=bias_rows[D_H // P : 2 * D_H // P, :],
+            in_=bias_update.rearrange("o (m p) -> (o m) p", p=P),
+        )
+        zeta_raw = consts.tile([P, 1], BF16)
+        nc.scalar.dma_start(out=zeta_raw[:], in_=zeta.rearrange("a b -> (a b)").partition_broadcast(P))
+        nu_raw = consts.tile([P, 1], BF16)
+        nc.scalar.dma_start(out=nu_raw[:], in_=nu.rearrange("a b -> (a b)").partition_broadcast(P))
+
+        zeta_sig = consts.tile([P, 1], F32)
+        nc.scalar.activation(out=zeta_sig[:], in_=zeta_raw[:], func=ACT.Sigmoid)
+        nu_sig = consts.tile([P, 1], F32)
+        nc.scalar.activation(out=nu_sig[:], in_=nu_raw[:], func=ACT.Sigmoid)
+        zeta_safe = consts.tile([P, 1], F32)
+        nc.vector.tensor_scalar(
+            out=zeta_safe[:], in0=zeta_sig[:], scalar1=TINY, scalar2=None, op0=ALU.max
+        )
+        zeta_inv = consts.tile([P, 1], F32)
+        nc.vector.reciprocal(out=zeta_inv[:], in_=zeta_safe[:])
+        ratio = consts.tile([P, 1], F32)
+        nc.vector.tensor_tensor(out=ratio[:], in0=nu_sig[:], in1=zeta_inv[:], op=ALU.mult)
+        neg_kappa = consts.tile([P, 1], F32)
+        nc.vector.tensor_scalar(
+            out=neg_kappa[:], in0=ratio[:], scalar1=-1.0, scalar2=-1.0, op0=ALU.mult, op1=ALU.add
+        )
+        neg_zeta = consts.tile([P, 1], F32)
+        nc.vector.tensor_scalar(
+            out=neg_zeta[:], in0=zeta_safe[:], scalar1=-1.0, scalar2=None, op0=ALU.mult
+        )
+        bias_rows_f32 = consts.tile([P, P], F32)
+        nc.vector.tensor_copy(out=bias_rows_f32[:], in_=bias_rows[:])
+        bias_cols = consts.tile([P, 2 * D_H // P], F32)
+
+        def flip_biases():
+            flipped = flip_banks.tile([P, P], F32, tag="flip")
+            nc.tensor.transpose(flipped[:], bias_rows_f32[:], ident[:])
+            nc.vector.tensor_copy(out=bias_cols[:], in_=flipped[:, 0 : 2 * D_H // P])
+
+        def flip_x(step, pair):
+            if pair == 0:
+                grouped = grouped_pool.tile([P, 4 * GROUP], BF16, align_bytes=64)
+                grouped_tiles[step] = grouped
+            x_words = x_tiles[step][:].rearrange("p j k -> p (j k)").bitcast(F32)
+            flipped = flip_banks.tile([P, 2, 2, P], F32, tag="flip")
+            for jj in range(2):
+                first = (2 * pair + jj) * WORDS
+                for u in range(2):
+                    nc.tensor.transpose(
+                        flipped[:, jj, u, :], x_words[:, first + u : first + WORDS : 2], ident[:]
+                    )
+            grouped_words = grouped_tiles[step][:].bitcast(F32)
+            grouped_words = grouped_words.rearrange("p (j b u) -> p j b u", j=ROWS, u=2)
+            nc.scalar.copy(
+                out=grouped_words[:, 2 * pair : 2 * pair + 2, :, :],
+                in_=flipped[:].rearrange("p j u b -> p j b u"),
+            )
+
+        def quantise_x(step):
+            codes = code_pool.tile([P, GROUP], U32, align_bytes=64)
+            scales = code_pool.tile([P, GROUP], U8, align_bytes=64)
+            nc.vector.quantize_mx(
+                out=codes[:].bitcast(FP8X4), scales=scales[:], in_=grouped_tiles[step][:]
+            )
+            quantised[step] = (codes, scales)
+
+        def open_unit(unit):
+            z_t = feature_pool.tile([P, TILES, GROUP], F32)
+            c_t = feature_pool.tile([P, TILES, GROUP], F32)
+            p_t = feature_pool.tile([P, TILES, GROUP], F32)
+            z_tiles[unit], c_tiles[unit], p_tiles[unit] = z_t, c_t, p_t
+
+        def gate_and_candidate(unit, t):
+            group, half = divmod(unit, HALVES)
+            m = half * TILES + t
+            acc = acc_banks.tile([P, GROUP], F32)
+            for operand in range(2):
+                codes, scales = quantised[2 * group + operand]
+                nc.tensor.matmul_mx(
+                    out=acc[:],
+                    lhsT=w_words[:, operand, 2 * P * m : 2 * P * (m + 1)].bitcast(FP4X4),
+                    lhsT_scale=w_planes[:, operand, P * m : P * (m + 1)],
+                    rhs=codes[:].bitcast(FP8X4),
+                    rhs_scale=scales[:],
+                    start=(operand == 0),
+                    stop=(operand == 1),
+                )
+            nc.scalar.activation(
+                out=z_tiles[unit][:, t, :], in_=acc[:], func=ACT.Sigmoid, bias=bias_cols[:, m : m + 1]
+            )
+            nc.scalar.activation(
+                out=c_tiles[unit][:, t, :],
+                in_=acc[:],
+                func=ACT.Tanh,
+                bias=bias_cols[:, D_H // P + m : D_H // P + m + 1],
+            )
+
+        def weigh_candidate_gpsimd(unit):
+            z_part = z_tiles[unit][:, 0:GPSIMD_TILES, :]
+            c_part = c_tiles[unit][:, 0:GPSIMD_TILES, :]
+            p_part = p_tiles[unit][:, 0:GPSIMD_TILES, :]
+            nc.gpsimd.tensor_scalar(
+                out=p_part, in0=z_part, scalar1=1.0, scalar2=neg_kappa[:, 0:1], op0=ALU.mult, op1=ALU.add
+            )
+            nc.gpsimd.tensor_tensor(out=p_part, in0=p_part, in1=c_part, op=ALU.mult)
+
+        def weigh_candidate_vector(unit):
+            for t in range(GPSIMD_TILES, TILES):
+                nc.vector.scalar_tensor_tensor(
+                    out=p_tiles[unit][:, t, :],
+                    in0=z_tiles[unit][:, t, :],
+                    scalar=neg_kappa[:, 0:1],
+                    in1=c_tiles[unit][:, t, :],
+                    op0=ALU.add,
+                    op1=ALU.mult,
+                )
+
+        def flip_unit(feature_major, j):
+            flipped = flip_banks.tile([P, HALF], F32, tag="flip")
+            for t in range(TILES):
+                nc.tensor.transpose(
+                    flipped[:, t * P : (t + 1) * P], feature_major[:, t, j * P : (j + 1) * P], ident[:]
+                )
+            return flipped
+
+        def keep_state(unit, j):
+            group, half = divmod(unit, HALVES)
+            if half == 0 and j == 0:
+                out_sb = out_pool.tile([P, ROWS, D_H], F32)
+                out_tiles[group] = out_sb
+            cols = slice(half * HALF, (half + 1) * HALF)
+            z_rows = flip_unit(z_tiles[unit], j)
+            nc.vector.tensor_tensor(
+                out=out_tiles[group][:, j, cols],
+                in0=z_rows[:],
+                in1=state_tiles[group][:, j, cols],
+                op=ALU.mult,
+            )
+
+        def add_candidate(unit, j):
+            group, half = divmod(unit, HALVES)
+            cols = slice(half * HALF, (half + 1) * HALF)
+            p_rows = flip_unit(p_tiles[unit], j)
+            nc.vector.scalar_tensor_tensor(
+                out=out_tiles[group][:, j, cols],
+                in0=p_rows[:],
+                scalar=neg_zeta[:, 0:1],
+                in1=out_tiles[group][:, j, cols],
+                op0=ALU.mult,
+                op1=ALU.add,
+            )
+            if half == HALVES - 1 and j % 2 == 1:
+                nc.sync.dma_start(
+                    out=group_rows(out, group)[:, j - 1 : j + 1, :],
+                    in_=out_tiles[group][:, j - 1 : j + 1, :],
+                )
+
+        for step in range(STEP_LEAD):
+            flip_x(step, 0)
+            flip_x(step, 1)
+            quantise_x(step)
+            if step == 1:
+                flip_biases()
+
+        for unit in range(N_UNITS + 1):
+            step = unit + STEP_LEAD
+            done = unit - 1
+            if unit % HALVES == 0:
+                group = unit // HALVES
+                if group + 3 < N_GROUPS:
+                    load_x(group + 3)
+                if group + 1 < N_GROUPS:
+                    load_state(group + 1)
+            if unit < N_UNITS:
+                open_unit(unit)
+                gate_and_candidate(unit, 0)
+                gate_and_candidate(unit, 1)
+            if step < N_STEPS:
+                flip_x(step, 0)
+            if done >= 0:
+                for j in range(ROWS):
+                    keep_state(done, j)
+            if unit < N_UNITS:
+                gate_and_candidate(unit, 2)
+                weigh_candidate_gpsimd(unit)
+                gate_and_candidate(unit, 3)
+            if step < N_STEPS:
+                flip_x(step, 1)
+            if done >= 0:
+                for j in range(ROWS):
+                    add_candidate(done, j)
+            if step < N_STEPS:
+                quantise_x(step)
+            if unit < N_UNITS:
+                weigh_candidate_vector(unit)

@@ -57,11 +57,12 @@ def tile_fastgrnncudacell_pa_t_kernel(
         grouped_pool = stack.enter_context(tc.tile_pool(name="grouped", bufs=2))
         code_pool = stack.enter_context(tc.tile_pool(name="codes", bufs=4))
         feature_pool = stack.enter_context(tc.tile_pool(name="feature_major", bufs=2))
-        acc_banks = stack.enter_context(tc.psum_pool(name="acc", bufs=3))
-        flip_banks = stack.enter_context(tc.psum_pool(name="flip", bufs=5))
+        acc_banks = stack.enter_context(tc.psum_pool(name="acc", bufs=2))
+        flip_banks = stack.enter_context(tc.psum_pool(name="flip", bufs=6))
         stack.enter_context(tc.manual_schedule())
 
         x_tiles = {}
+        x_banks = {}
         grouped_tiles = {}
         quantised = {}
         state_tiles = {}
@@ -146,24 +147,27 @@ def tile_fastgrnncudacell_pa_t_kernel(
             nc.tensor.transpose(flipped[:], bias_rows_f32[:], ident[:])
             nc.vector.tensor_copy(out=bias_cols[:], in_=flipped[:, 0 : 2 * D_H // P])
 
-        def flip_x(step, pair):
-            if pair == 0:
+        def flip_x(step, j):
+            if j == 0:
                 grouped = grouped_pool.tile([P, 4 * GROUP], BF16, align_bytes=64)
                 grouped_tiles[step] = grouped
+            if j % 2 == 0:
+                flipped = flip_banks.tile([P, 2, 2, P], F32, tag="flip")
+                x_banks[step] = flipped
             x_words = x_tiles[step][:].rearrange("p j k -> p (j k)").bitcast(F32)
-            flipped = flip_banks.tile([P, 2, 2, P], F32, tag="flip")
-            for jj in range(2):
-                first = (2 * pair + jj) * WORDS
-                for u in range(2):
-                    nc.tensor.transpose(
-                        flipped[:, jj, u, :], x_words[:, first + u : first + WORDS : 2], ident[:]
-                    )
-            grouped_words = grouped_tiles[step][:].bitcast(F32)
-            grouped_words = grouped_words.rearrange("p (j b u) -> p j b u", j=ROWS, u=2)
-            nc.scalar.copy(
-                out=grouped_words[:, 2 * pair : 2 * pair + 2, :, :],
-                in_=flipped[:].rearrange("p j u b -> p j b u"),
-            )
+            for u in range(2):
+                nc.tensor.transpose(
+                    x_banks[step][:, j % 2, u, :],
+                    x_words[:, j * WORDS + u : (j + 1) * WORDS : 2],
+                    ident[:],
+                )
+            if j % 2 == 1:
+                grouped_words = grouped_tiles[step][:].bitcast(F32)
+                grouped_words = grouped_words.rearrange("p (j b u) -> p j b u", j=ROWS, u=2)
+                nc.scalar.copy(
+                    out=grouped_words[:, j - 1 : j + 1, :, :],
+                    in_=x_banks[step][:].rearrange("p j u b -> p j b u"),
+                )
 
         def quantise_x(step):
             codes = code_pool.tile([P, GROUP], U32, align_bytes=64)
@@ -264,12 +268,11 @@ def tile_fastgrnncudacell_pa_t_kernel(
                     in_=out_tiles[group][:, j - 1 : j + 1, :],
                 )
 
+        flip_biases()
         for step in range(STEP_LEAD):
-            flip_x(step, 0)
-            flip_x(step, 1)
+            for j in range(ROWS):
+                flip_x(step, j)
             quantise_x(step)
-            if step == 1:
-                flip_biases()
 
         for unit in range(N_UNITS + 1):
             step = unit + STEP_LEAD
@@ -282,22 +285,19 @@ def tile_fastgrnncudacell_pa_t_kernel(
                     load_state(group + 1)
             if unit < N_UNITS:
                 open_unit(unit)
-                gate_and_candidate(unit, 0)
-                gate_and_candidate(unit, 1)
-            if step < N_STEPS:
-                flip_x(step, 0)
-            if done >= 0:
-                for j in range(ROWS):
-                    keep_state(done, j)
-            if unit < N_UNITS:
-                gate_and_candidate(unit, 2)
-                weigh_candidate_gpsimd(unit)
-                gate_and_candidate(unit, 3)
-            if step < N_STEPS:
-                flip_x(step, 1)
-            if done >= 0:
-                for j in range(ROWS):
-                    add_candidate(done, j)
+            for quarter in range(4):
+                if unit < N_UNITS:
+                    gate_and_candidate(unit, quarter)
+                if step < N_STEPS:
+                    flip_x(step, quarter)
+                if done >= 0 and quarter < 2:
+                    keep_state(done, 2 * quarter)
+                    keep_state(done, 2 * quarter + 1)
+                if done >= 0 and quarter >= 2:
+                    add_candidate(done, 2 * quarter - 4)
+                    add_candidate(done, 2 * quarter - 3)
+                if unit < N_UNITS and quarter == GPSIMD_TILES - 1:
+                    weigh_candidate_gpsimd(unit)
             if step < N_STEPS:
                 quantise_x(step)
             if unit < N_UNITS:

@@ -27,7 +27,7 @@ HALVES = D_H // HALF
 N_UNITS = N_GROUPS * HALVES
 N_STEPS = 2 * N_GROUPS
 STEP_LEAD = 3
-GPSIMD_TILES = 3
+GPSIMD_TILES = 2
 TINY = 1e-30
 
 FLOPS = 2 * BATCH * D_H * 2 * RANK
@@ -57,12 +57,11 @@ def tile_fastgrnncudacell_pa_t_kernel(
         grouped_pool = stack.enter_context(tc.tile_pool(name="grouped", bufs=2))
         code_pool = stack.enter_context(tc.tile_pool(name="codes", bufs=4))
         feature_pool = stack.enter_context(tc.tile_pool(name="feature_major", bufs=2))
-        acc_banks = stack.enter_context(tc.psum_pool(name="acc", bufs=2))
-        flip_banks = stack.enter_context(tc.psum_pool(name="flip", bufs=6))
+        acc_banks = stack.enter_context(tc.psum_pool(name="acc", bufs=3))
+        flip_banks = stack.enter_context(tc.psum_pool(name="flip", bufs=5))
         stack.enter_context(tc.manual_schedule())
 
         x_tiles = {}
-        x_banks = {}
         grouped_tiles = {}
         quantised = {}
         state_tiles = {}
@@ -147,27 +146,24 @@ def tile_fastgrnncudacell_pa_t_kernel(
             nc.tensor.transpose(flipped[:], bias_rows_f32[:], ident[:])
             nc.vector.tensor_copy(out=bias_cols[:], in_=flipped[:, 0 : 2 * D_H // P])
 
-        def flip_x(step, j):
-            if j == 0:
+        def flip_x(step, pair):
+            if pair == 0:
                 grouped = grouped_pool.tile([P, 4 * GROUP], BF16, align_bytes=64)
                 grouped_tiles[step] = grouped
-            if j % 2 == 0:
-                flipped = flip_banks.tile([P, 2, 2, P], F32, tag="flip")
-                x_banks[step] = flipped
             x_words = x_tiles[step][:].rearrange("p j k -> p (j k)").bitcast(F32)
-            for u in range(2):
-                nc.tensor.transpose(
-                    x_banks[step][:, j % 2, u, :],
-                    x_words[:, j * WORDS + u : (j + 1) * WORDS : 2],
-                    ident[:],
-                )
-            if j % 2 == 1:
-                grouped_words = grouped_tiles[step][:].bitcast(F32)
-                grouped_words = grouped_words.rearrange("p (j b u) -> p j b u", j=ROWS, u=2)
-                nc.scalar.copy(
-                    out=grouped_words[:, j - 1 : j + 1, :, :],
-                    in_=x_banks[step][:].rearrange("p j u b -> p j b u"),
-                )
+            flipped = flip_banks.tile([P, 2, 2, P], F32, tag="flip")
+            for jj in range(2):
+                first = (2 * pair + jj) * WORDS
+                for u in range(2):
+                    nc.tensor.transpose(
+                        flipped[:, jj, u, :], x_words[:, first + u : first + WORDS : 2], ident[:]
+                    )
+            grouped_words = grouped_tiles[step][:].bitcast(F32)
+            grouped_words = grouped_words.rearrange("p (j b u) -> p j b u", j=ROWS, u=2)
+            nc.scalar.copy(
+                out=grouped_words[:, 2 * pair : 2 * pair + 2, :, :],
+                in_=flipped[:].rearrange("p j u b -> p j b u"),
+            )
 
         def quantise_x(step):
             codes = code_pool.tile([P, GROUP], U32, align_bytes=64)
@@ -268,11 +264,12 @@ def tile_fastgrnncudacell_pa_t_kernel(
                     in_=out_tiles[group][:, j - 1 : j + 1, :],
                 )
 
-        flip_biases()
         for step in range(STEP_LEAD):
-            for j in range(ROWS):
-                flip_x(step, j)
+            flip_x(step, 0)
+            flip_x(step, 1)
             quantise_x(step)
+            if step == 1:
+                flip_biases()
 
         for unit in range(N_UNITS + 1):
             step = unit + STEP_LEAD
@@ -285,19 +282,22 @@ def tile_fastgrnncudacell_pa_t_kernel(
                     load_state(group + 1)
             if unit < N_UNITS:
                 open_unit(unit)
-            for quarter in range(4):
-                if unit < N_UNITS:
-                    gate_and_candidate(unit, quarter)
-                if step < N_STEPS:
-                    flip_x(step, quarter)
-                if done >= 0 and quarter < 2:
-                    keep_state(done, 2 * quarter)
-                    keep_state(done, 2 * quarter + 1)
-                if done >= 0 and quarter >= 2:
-                    add_candidate(done, 2 * quarter - 4)
-                    add_candidate(done, 2 * quarter - 3)
-                if unit < N_UNITS and quarter == GPSIMD_TILES - 1:
-                    weigh_candidate_gpsimd(unit)
+                gate_and_candidate(unit, 0)
+                gate_and_candidate(unit, 1)
+            if step < N_STEPS:
+                flip_x(step, 0)
+            if done >= 0:
+                for j in range(ROWS):
+                    keep_state(done, j)
+            if unit < N_UNITS:
+                gate_and_candidate(unit, 2)
+                weigh_candidate_gpsimd(unit)
+                gate_and_candidate(unit, 3)
+            if step < N_STEPS:
+                flip_x(step, 1)
+            if done >= 0:
+                for j in range(ROWS):
+                    add_candidate(done, j)
             if step < N_STEPS:
                 quantise_x(step)
             if unit < N_UNITS:

@@ -173,6 +173,11 @@ def tile_fastgrnncudacell_pa_t_kernel(
             )
             quantised[step] = (codes, scales)
 
+        def prepare_x(step):
+            flip_x(step, 0)
+            flip_x(step, 1)
+            quantise_x(step)
+
         def open_unit(unit):
             z_t = feature_pool.tile([P, TILES, GROUP], F32)
             c_t = feature_pool.tile([P, TILES, GROUP], F32)
@@ -214,15 +219,14 @@ def tile_fastgrnncudacell_pa_t_kernel(
             nc.gpsimd.tensor_tensor(out=p_part, in0=p_part, in1=c_part, op=ALU.mult)
 
         def weigh_candidate_vector(unit):
-            for t in range(GPSIMD_TILES, TILES):
-                nc.vector.scalar_tensor_tensor(
-                    out=p_tiles[unit][:, t, :],
-                    in0=z_tiles[unit][:, t, :],
-                    scalar=neg_kappa[:, 0:1],
-                    in1=c_tiles[unit][:, t, :],
-                    op0=ALU.add,
-                    op1=ALU.mult,
-                )
+            nc.vector.scalar_tensor_tensor(
+                out=p_tiles[unit][:, GPSIMD_TILES:TILES, :],
+                in0=z_tiles[unit][:, GPSIMD_TILES:TILES, :],
+                scalar=neg_kappa[:, 0:1],
+                in1=c_tiles[unit][:, GPSIMD_TILES:TILES, :],
+                op0=ALU.add,
+                op1=ALU.mult,
+            )
 
         def flip_unit(feature_major, j):
             flipped = flip_banks.tile([P, HALF], F32, tag="flip")
@@ -258,18 +262,14 @@ def tile_fastgrnncudacell_pa_t_kernel(
                 op0=ALU.mult,
                 op1=ALU.add,
             )
-            if half == HALVES - 1 and j % 2 == 1:
+            if half == HALVES - 1:
                 nc.sync.dma_start(
-                    out=group_rows(out, group)[:, j - 1 : j + 1, :],
-                    in_=out_tiles[group][:, j - 1 : j + 1, :],
+                    out=group_rows(out, group)[:, j, :], in_=out_tiles[group][:, j, :]
                 )
 
-        for step in range(STEP_LEAD):
-            flip_x(step, 0)
-            flip_x(step, 1)
-            quantise_x(step)
-            if step == 1:
-                flip_biases()
+        prepare_x(0)
+        prepare_x(1)
+        flip_biases()
 
         for unit in range(N_UNITS + 1):
             step = unit + STEP_LEAD
@@ -284,14 +284,16 @@ def tile_fastgrnncudacell_pa_t_kernel(
                 open_unit(unit)
                 gate_and_candidate(unit, 0)
                 gate_and_candidate(unit, 1)
+                weigh_candidate_gpsimd(unit)
             if step < N_STEPS:
                 flip_x(step, 0)
             if done >= 0:
                 for j in range(ROWS):
                     keep_state(done, j)
+            else:
+                prepare_x(STEP_LEAD - 1)
             if unit < N_UNITS:
                 gate_and_candidate(unit, 2)
-                weigh_candidate_gpsimd(unit)
                 gate_and_candidate(unit, 3)
             if step < N_STEPS:
                 flip_x(step, 1)

@@ -88,9 +88,22 @@ def tile_fastgrnncudacell_pa_t_kernel(
         w_planes = consts.tile([P, 2, D_H], U8, align_bytes=64)
         nc.vector.memset(w_planes[:].rearrange("p o n -> p (o n)").bitcast(I32), 0)
         bias_rows = consts.tile([P, P], BF16)
-        nc.vector.memset(bias_rows[:], 0.0)
+        bias_rows_f32 = consts.tile([P, P], F32)
+        nc.vector.memset(bias_rows_f32[:], 0.0)
         ident = consts.tile([P, P], F32)
         make_identity(nc, ident[:])
+
+        nc.sync.dma_start(
+            out=bias_rows[0 : D_H // P, :], in_=bias_gate.rearrange("o (m p) -> (o m) p", p=P)
+        )
+        nc.sync.dma_start(
+            out=bias_rows[D_H // P : 2 * D_H // P, :],
+            in_=bias_update.rearrange("o (m p) -> (o m) p", p=P),
+        )
+        zeta_raw = consts.tile([P, 1], BF16)
+        nc.sync.dma_start(out=zeta_raw[:], in_=zeta.rearrange("a b -> (a b)").partition_broadcast(P))
+        nu_raw = consts.tile([P, 1], BF16)
+        nc.sync.dma_start(out=nu_raw[:], in_=nu.rearrange("a b -> (a b)").partition_broadcast(P))
 
         load_x(0)
         w_words = consts.tile([P, 2, 2 * D_H], U8, align_bytes=64)
@@ -105,17 +118,10 @@ def tile_fastgrnncudacell_pa_t_kernel(
         load_state(0)
         load_x(2)
 
-        nc.scalar.dma_start(
-            out=bias_rows[0 : D_H // P, :], in_=bias_gate.rearrange("o (m p) -> (o m) p", p=P)
-        )
-        nc.scalar.dma_start(
-            out=bias_rows[D_H // P : 2 * D_H // P, :],
-            in_=bias_update.rearrange("o (m p) -> (o m) p", p=P),
-        )
-        zeta_raw = consts.tile([P, 1], BF16)
-        nc.scalar.dma_start(out=zeta_raw[:], in_=zeta.rearrange("a b -> (a b)").partition_broadcast(P))
-        nu_raw = consts.tile([P, 1], BF16)
-        nc.scalar.dma_start(out=nu_raw[:], in_=nu.rearrange("a b -> (a b)").partition_broadcast(P))
+        warm = consts.tile([P, 1], F32)
+        nc.vector.memset(warm[:], 0.0)
+        nc.scalar.activation(out=warm[:], in_=warm[:], func=ACT.Sigmoid)
+        nc.vector.tensor_copy(out=bias_rows_f32[0 : 2 * D_H // P, :], in_=bias_rows[0 : 2 * D_H // P, :])
 
         zeta_sig = consts.tile([P, 1], F32)
         nc.scalar.activation(out=zeta_sig[:], in_=zeta_raw[:], func=ACT.Sigmoid)
@@ -137,8 +143,6 @@ def tile_fastgrnncudacell_pa_t_kernel(
         nc.vector.tensor_scalar(
             out=neg_zeta[:], in0=zeta_safe[:], scalar1=-1.0, scalar2=None, op0=ALU.mult
         )
-        bias_rows_f32 = consts.tile([P, P], F32)
-        nc.vector.tensor_copy(out=bias_rows_f32[:], in_=bias_rows[:])
         bias_cols = consts.tile([P, 2 * D_H // P], F32)
 
         def flip_biases():
@@ -262,14 +266,18 @@ def tile_fastgrnncudacell_pa_t_kernel(
                 op0=ALU.mult,
                 op1=ALU.add,
             )
-            if half == HALVES - 1:
+            if group == N_GROUPS - 1:
+                nc.sync.dma_start(
+                    out=group_rows(out, group)[:, j, cols], in_=out_tiles[group][:, j, cols]
+                )
+            elif half == HALVES - 1:
                 nc.sync.dma_start(
                     out=group_rows(out, group)[:, j, :], in_=out_tiles[group][:, j, :]
                 )
 
+        flip_biases()
         prepare_x(0)
         prepare_x(1)
-        flip_biases()
 
         for unit in range(N_UNITS + 1):
             step = unit + STEP_LEAD

from contextlib import ExitStack

import concourse.mybir as mybir
from concourse.masks import make_identity

F32 = mybir.dt.float32
BF16 = mybir.dt.bfloat16
I32 = mybir.dt.int32
U32 = mybir.dt.uint32
U8 = mybir.dt.uint8
FP8X4 = mybir.dt.float8_e4m3fn_x4
FP4X4 = mybir.dt.float4_e2m1fn_x4
ACT = mybir.ActivationFunctionType
ALU = mybir.AluOpType

P = 128
BATCH = 4096
RANK = 512
D_H = 1024
WORDS = RANK // 2
GROUP = 512
ROWS = GROUP // P
N_GROUPS = BATCH // GROUP
HALF = 512
TILES = HALF // P
HALVES = D_H // HALF
N_UNITS = N_GROUPS * HALVES
N_STEPS = 2 * N_GROUPS
STEP_LEAD = 3
GPSIMD_TILES = 2
TINY = 1e-30

FLOPS = 2 * BATCH * D_H * 2 * RANK


def tile_fastgrnncudacell_pa_t_kernel(
    tc,
    wx_r,
    uh_r,
    state,
    W2_words,
    W2_scales,
    U2_words,
    U2_scales,
    bias_gate,
    bias_update,
    zeta,
    nu,
    out,
):
    nc = tc.nc
    with ExitStack() as stack:
        consts = stack.enter_context(tc.tile_pool(name="consts", bufs=1))
        x_pool = stack.enter_context(tc.tile_pool(name="x", bufs=6))
        state_pool = stack.enter_context(tc.tile_pool(name="state", bufs=3))
        out_pool = stack.enter_context(tc.tile_pool(name="out", bufs=2))
        grouped_pool = stack.enter_context(tc.tile_pool(name="grouped", bufs=2))
        code_pool = stack.enter_context(tc.tile_pool(name="codes", bufs=4))
        feature_pool = stack.enter_context(tc.tile_pool(name="feature_major", bufs=2))
        acc_banks = stack.enter_context(tc.psum_pool(name="acc", bufs=3))
        flip_banks = stack.enter_context(tc.psum_pool(name="flip", bufs=5))
        stack.enter_context(tc.manual_schedule())

        x_tiles = {}
        grouped_tiles = {}
        quantised = {}
        state_tiles = {}
        out_tiles = {}
        z_tiles = {}
        c_tiles = {}
        p_tiles = {}

        def group_rows(dram, group):
            rows = dram[group * GROUP : (group + 1) * GROUP, :]
            return rows.rearrange("(p j) c -> p j c", j=ROWS)

        def load_x(group):
            for operand, source in enumerate((wx_r, uh_r)):
                x_sb = x_pool.tile([P, ROWS, RANK], BF16)
                nc.sync.dma_start(out=x_sb[:], in_=group_rows(source, group))
                x_tiles[2 * group + operand] = x_sb

        def load_state(group):
            state_sb = state_pool.tile([P, ROWS, D_H], BF16)
            nc.sync.dma_start(out=state_sb[:], in_=group_rows(state, group))
            state_tiles[group] = state_sb

        w_planes = consts.tile([P, 2, D_H], U8, align_bytes=64)
        nc.vector.memset(w_planes[:].rearrange("p o n -> p (o n)").bitcast(I32), 0)
        bias_rows = consts.tile([P, P], BF16)
        bias_rows_f32 = consts.tile([P, P], F32)
        nc.vector.memset(bias_rows_f32[:], 0.0)
        ident = consts.tile([P, P], F32)
        make_identity(nc, ident[:])

        nc.sync.dma_start(
            out=bias_rows[0 : D_H // P, :], in_=bias_gate.rearrange("o (m p) -> (o m) p", p=P)
        )
        nc.sync.dma_start(
            out=bias_rows[D_H // P : 2 * D_H // P, :],
            in_=bias_update.rearrange("o (m p) -> (o m) p", p=P),
        )
        zeta_raw = consts.tile([P, 1], BF16)
        nc.sync.dma_start(out=zeta_raw[:], in_=zeta.rearrange("a b -> (a b)").partition_broadcast(P))
        nu_raw = consts.tile([P, 1], BF16)
        nc.sync.dma_start(out=nu_raw[:], in_=nu.rearrange("a b -> (a b)").partition_broadcast(P))

        load_x(0)
        w_words = consts.tile([P, 2, 2 * D_H], U8, align_bytes=64)
        for operand, (words, scales) in enumerate(((W2_words, W2_scales), (U2_words, U2_scales))):
            nc.sync.dma_start(out=w_words[:, operand, :].bitcast(I32), in_=words[0].bitcast(I32))
            for quadrant in range(4):
                nc.sync.dma_start(
                    out=w_planes[32 * quadrant : 32 * quadrant + 4, operand, :].bitcast(I32),
                    in_=scales[0, 4 * quadrant : 4 * quadrant + 4, :].bitcast(I32),
                )
        load_x(1)
        load_state(0)
        load_x(2)

        warm = consts.tile([P, 1], F32)
        nc.vector.memset(warm[:], 0.0)
        nc.scalar.activation(out=warm[:], in_=warm[:], func=ACT.Sigmoid)
        nc.vector.tensor_copy(out=bias_rows_f32[0 : 2 * D_H // P, :], in_=bias_rows[0 : 2 * D_H // P, :])

        zeta_sig = consts.tile([P, 1], F32)
        nc.scalar.activation(out=zeta_sig[:], in_=zeta_raw[:], func=ACT.Sigmoid)
        nu_sig = consts.tile([P, 1], F32)
        nc.scalar.activation(out=nu_sig[:], in_=nu_raw[:], func=ACT.Sigmoid)
        zeta_safe = consts.tile([P, 1], F32)
        nc.vector.tensor_scalar(
            out=zeta_safe[:], in0=zeta_sig[:], scalar1=TINY, scalar2=None, op0=ALU.max
        )
        zeta_inv = consts.tile([P, 1], F32)
        nc.vector.reciprocal(out=zeta_inv[:], in_=zeta_safe[:])
        ratio = consts.tile([P, 1], F32)
        nc.vector.tensor_tensor(out=ratio[:], in0=nu_sig[:], in1=zeta_inv[:], op=ALU.mult)
        neg_kappa = consts.tile([P, 1], F32)
        nc.vector.tensor_scalar(
            out=neg_kappa[:], in0=ratio[:], scalar1=-1.0, scalar2=-1.0, op0=ALU.mult, op1=ALU.add
        )
        neg_zeta = consts.tile([P, 1], F32)
        nc.vector.tensor_scalar(
            out=neg_zeta[:], in0=zeta_safe[:], scalar1=-1.0, scalar2=None, op0=ALU.mult
        )
        bias_cols = consts.tile([P, 2 * D_H // P], F32)

        def flip_biases():
            flipped = flip_banks.tile([P, P], F32, tag="flip")
            nc.tensor.transpose(flipped[:], bias_rows_f32[:], ident[:])
            nc.vector.tensor_copy(out=bias_cols[:], in_=flipped[:, 0 : 2 * D_H // P])

        def flip_x(step, pair):
            if pair == 0:
                grouped = grouped_pool.tile([P, 4 * GROUP], BF16, align_bytes=64)
                grouped_tiles[step] = grouped
            x_words = x_tiles[step][:].rearrange("p j k -> p (j k)").bitcast(F32)
            flipped = flip_banks.tile([P, 2, 2, P], F32, tag="flip")
            for jj in range(2):
                first = (2 * pair + jj) * WORDS
                for u in range(2):
                    nc.tensor.transpose(
                        flipped[:, jj, u, :], x_words[:, first + u : first + WORDS : 2], ident[:]
                    )
            grouped_words = grouped_tiles[step][:].bitcast(F32)
            grouped_words = grouped_words.rearrange("p (j b u) -> p j b u", j=ROWS, u=2)
            nc.scalar.copy(
                out=grouped_words[:, 2 * pair : 2 * pair + 2, :, :],
                in_=flipped[:].rearrange("p j u b -> p j b u"),
            )

        def quantise_x(step):
            codes = code_pool.tile([P, GROUP], U32, align_bytes=64)
            scales = code_pool.tile([P, GROUP], U8, align_bytes=64)
            nc.vector.quantize_mx(
                out=codes[:].bitcast(FP8X4), scales=scales[:], in_=grouped_tiles[step][:]
            )
            quantised[step] = (codes, scales)

        def prepare_x(step):
            flip_x(step, 0)
            flip_x(step, 1)
            quantise_x(step)

        def open_unit(unit):
            z_t = feature_pool.tile([P, TILES, GROUP], F32)
            c_t = feature_pool.tile([P, TILES, GROUP], F32)
            p_t = feature_pool.tile([P, TILES, GROUP], F32)
            z_tiles[unit], c_tiles[unit], p_tiles[unit] = z_t, c_t, p_t

        def gate_and_candidate(unit, t):
            group, half = divmod(unit, HALVES)
            m = half * TILES + t
            acc = acc_banks.tile([P, GROUP], F32)
            for operand in range(2):
                codes, scales = quantised[2 * group + operand]
                nc.tensor.matmul_mx(
                    out=acc[:],
                    lhsT=w_words[:, operand, 2 * P * m : 2 * P * (m + 1)].bitcast(FP4X4),
                    lhsT_scale=w_planes[:, operand, P * m : P * (m + 1)],
                    rhs=codes[:].bitcast(FP8X4),
                    rhs_scale=scales[:],
                    start=(operand == 0),
                    stop=(operand == 1),
                )
            nc.scalar.activation(
                out=z_tiles[unit][:, t, :], in_=acc[:], func=ACT.Sigmoid, bias=bias_cols[:, m : m + 1]
            )
            nc.scalar.activation(
                out=c_tiles[unit][:, t, :],
                in_=acc[:],
                func=ACT.Tanh,
                bias=bias_cols[:, D_H // P + m : D_H // P + m + 1],
            )

        def weigh_candidate_gpsimd(unit):
            z_part = z_tiles[unit][:, 0:GPSIMD_TILES, :]
            c_part = c_tiles[unit][:, 0:GPSIMD_TILES, :]
            p_part = p_tiles[unit][:, 0:GPSIMD_TILES, :]
            nc.gpsimd.tensor_scalar(
                out=p_part, in0=z_part, scalar1=1.0, scalar2=neg_kappa[:, 0:1], op0=ALU.mult, op1=ALU.add
            )
            nc.gpsimd.tensor_tensor(out=p_part, in0=p_part, in1=c_part, op=ALU.mult)

        def weigh_candidate_vector(unit):
            nc.vector.scalar_tensor_tensor(
                out=p_tiles[unit][:, GPSIMD_TILES:TILES, :],
                in0=z_tiles[unit][:, GPSIMD_TILES:TILES, :],
                scalar=neg_kappa[:, 0:1],
                in1=c_tiles[unit][:, GPSIMD_TILES:TILES, :],
                op0=ALU.add,
                op1=ALU.mult,
            )

        def flip_unit(feature_major, j):
            flipped = flip_banks.tile([P, HALF], F32, tag="flip")
            for t in range(TILES):
                nc.tensor.transpose(
                    flipped[:, t * P : (t + 1) * P], feature_major[:, t, j * P : (j + 1) * P], ident[:]
                )
            return flipped

        def keep_state(unit, j):
            group, half = divmod(unit, HALVES)
            if half == 0 and j == 0:
                out_sb = out_pool.tile([P, ROWS, D_H], F32)
                out_tiles[group] = out_sb
            cols = slice(half * HALF, (half + 1) * HALF)
            z_rows = flip_unit(z_tiles[unit], j)
            nc.vector.tensor_tensor(
                out=out_tiles[group][:, j, cols],
                in0=z_rows[:],
                in1=state_tiles[group][:, j, cols],
                op=ALU.mult,
            )

        def add_candidate(unit, j):
            group, half = divmod(unit, HALVES)
            cols = slice(half * HALF, (half + 1) * HALF)
            p_rows = flip_unit(p_tiles[unit], j)
            nc.vector.scalar_tensor_tensor(
                out=out_tiles[group][:, j, cols],
                in0=p_rows[:],
                scalar=neg_zeta[:, 0:1],
                in1=out_tiles[group][:, j, cols],
                op0=ALU.mult,
                op1=ALU.add,
            )
            if group == N_GROUPS - 1:
                nc.sync.dma_start(
                    out=group_rows(out, group)[:, j, cols], in_=out_tiles[group][:, j, cols]
                )
            elif half == HALVES - 1:
                nc.sync.dma_start(
                    out=group_rows(out, group)[:, j, :], in_=out_tiles[group][:, j, :]
                )

        flip_biases()
        prepare_x(0)
        prepare_x(1)

        for unit in range(N_UNITS + 1):
            step = unit + STEP_LEAD
            done = unit - 1
            if unit % HALVES == 0:
                group = unit // HALVES
                if group + 3 < N_GROUPS:
                    load_x(group + 3)
                if group + 1 < N_GROUPS:
                    load_state(group + 1)
            if unit < N_UNITS:
                open_unit(unit)
                gate_and_candidate(unit, 0)
                gate_and_candidate(unit, 1)
                weigh_candidate_gpsimd(unit)
            if step < N_STEPS:
                flip_x(step, 0)
            if done >= 0:
                for j in range(ROWS):
                    keep_state(done, j)
            else:
                prepare_x(STEP_LEAD - 1)
            if unit < N_UNITS:
                gate_and_candidate(unit, 2)
                gate_and_candidate(unit, 3)
            if step < N_STEPS:
                flip_x(step, 1)
            if done >= 0:
                for j in range(ROWS):
                    add_candidate(done, j)
            if step < N_STEPS:
                quantise_x(step)
            if unit < N_UNITS:
                weigh_candidate_vector(unit)
